import numpy as np
import ml_dtypes

BF16 = ml_dtypes.bfloat16


def bf(x):
    return np.asarray(x, np.float32).astype(BF16)


def f32(x):
    return np.asarray(x, np.float32)


def f64(x):
    return np.asarray(x).astype(np.float64)


def striped(idx):
    return np.tile(idx.reshape(-1, 16).T, (8, 1))


C, S, A, M, H, N = 128, 1024, 8, 128, 512, 8192


def setup_inputs():
    x = f32(np.random.standard_normal((C, S)))
    dist = f32(np.tile(np.random.random_sample((1, N)), (C, 1)))
    w = bf(np.random.standard_normal((C + C, M)) / np.sqrt(C))
    b = f32(0.1 * np.random.standard_normal((M, 1)))
    idx = np.concatenate([np.random.permutation(S)[:H] for _ in range(N // H)])
    return {"x": x, "dist": dist, "w": w, "b": b, "offs": striped(idx)}


def reference(x, dist, w, b, offs):
    idx = offs[:16].T.reshape(-1)
    msg = f64(x)[:, idx] * f64(dist)
    pre = f64(w)[:C].T @ msg
    own = f64(w)[C:].T @ f64(x) + f64(b)
    hid = np.maximum(pre.reshape(M, A, S) + own[:, None, :], 0.0)
    return hid.mean(axis=1)

@@ -1,0 +1,75 @@
+import concourse.mybir as mybir
+
+F32 = mybir.dt.float32
+BF16 = mybir.dt.bfloat16
+U16 = mybir.dt.uint16
+MULT = mybir.AluOpType.mult
+ADD = mybir.AluOpType.add
+COPY = mybir.ActivationFunctionType.Copy
+RELU = mybir.ActivationFunctionType.Relu
+
+FEATURES = 128
+NODES = 1024
+ANCHORS = 8
+PIECE = 512
+HALVES = NODES // PIECE
+ENTRIES = ANCHORS * NODES
+
+FLOPS = 2 * FEATURES * FEATURES * (ENTRIES + NODES)
+
+
+def tile_pgnn_kernel(tc, x, dist, w, b, offs, out):
+    nc = tc.nc
+    with (
+        tc.tile_pool(name="held", bufs=1) as held,
+        tc.tile_pool(name="ring", bufs=4) as ring,
+        tc.psum_pool(name="psum", bufs=4) as psum,
+    ):
+        offsets = held.tile([FEATURES, ENTRIES // 16], U16, name="offsets")
+        nc.sync.dma_start(offsets[:], offs)
+        nodes = held.tile([FEATURES, NODES], F32, name="nodes")
+        nc.scalar.dma_start(nodes[:], x)
+        w_msg = held.tile([FEATURES, FEATURES], BF16, name="w_msg")
+        nc.scalar.dma_start(w_msg[:], w[0:FEATURES, :])
+        w_own = held.tile([FEATURES, FEATURES], BF16, name="w_own")
+        nc.scalar.dma_start(w_own[:], w[FEATURES : 2 * FEATURES, :])
+        bias = held.tile([FEATURES, 1], F32, name="bias")
+        nc.scalar.dma_start(bias[:], b)
+
+        pieces = [(half, anchor) for half in range(HALVES) for anchor in range(ANCHORS)]
+
+        scores = {}
+        for half, anchor in pieces:
+            first = anchor * NODES + half * PIECE
+            scores[half, anchor] = held.tile([FEATURES, PIECE], F32, name=f"scores_{half}_{anchor}")
+            nc.sync.dma_start(scores[half, anchor][:], dist[:, first : first + PIECE])
+
+        nodes_bf = held.tile([FEATURES, NODES], BF16, name="nodes_bf")
+        nc.scalar.activation(nodes_bf[:], nodes[:], COPY)
+        bias_8th = held.tile([FEATURES, 1], F32, name="bias_8th")
+        nc.scalar.mul(bias_8th[:], bias[:], 1.0 / ANCHORS)
+
+        for half, anchor in pieces:
+            first = anchor * NODES + half * PIECE
+            own_columns = nodes_bf[:, half * PIECE : (half + 1) * PIECE]
+
+            picked = nodes[:].indirect(offsets[:, first // 16 : (first + PIECE) // 16])
+            weighted = ring.tile([FEATURES, PIECE], F32, name="weighted")
+            nc.vector.tensor_tensor(weighted[:], picked, scores[half, anchor][:], MULT)
+
+            message = ring.tile([FEATURES, PIECE], BF16, name="message")
+            nc.scalar.activation(message[:], weighted[:], COPY)
+
+            pre = psum.tile([FEATURES, PIECE], F32, name="pre")
+            nc.tensor.matmul(pre[:], w_own[:], own_columns, start=True, stop=False)
+            nc.tensor.matmul(pre[:], w_msg[:], message[:], start=False, stop=True)
+
+            if anchor == 0:
+                mean = ring.tile([FEATURES, PIECE], F32, name="mean")
+                nc.scalar.activation(mean[:], pre[:], RELU, bias=bias_8th[:], scale=1.0 / ANCHORS)
+            else:
+                hidden = ring.tile([FEATURES, PIECE], F32, name="hidden")
+                nc.scalar.activation(hidden[:], pre[:], RELU, bias=bias_8th[:], scale=1.0 / ANCHORS)
+                nc.vector.tensor_tensor(mean[:], mean[:], hidden[:], ADD)
+            if anchor == ANCHORS - 1:
+                nc.sync.dma_start(out[:, half * PIECE : (half + 1) * PIECE], mean[:])

@@ -1,4 +1,5 @@
 import concourse.mybir as mybir
+from concourse.masks import make_identity
 
 F32 = mybir.dt.float32
 BF16 = mybir.dt.bfloat16
@@ -14,6 +15,7 @@ ANCHORS = 8
 PIECE = 512
 HALVES = NODES // PIECE
 ENTRIES = ANCHORS * NODES
+SUMMED_BY_TENSOR = 6
 
 FLOPS = 2 * FEATURES * FEATURES * (ENTRIES + NODES)
 
@@ -24,6 +26,7 @@ def tile_pgnn_kernel(tc, x, dist, w, b, offs, out):
         tc.tile_pool(name="held", bufs=1) as held,
         tc.tile_pool(name="ring", bufs=4) as ring,
         tc.psum_pool(name="psum", bufs=4) as psum,
+        tc.psum_pool(name="sums", bufs=HALVES) as sums,
     ):
         offsets = held.tile([FEATURES, ENTRIES // 16], U16, name="offsets")
         nc.sync.dma_start(offsets[:], offs)
@@ -49,6 +52,9 @@ def tile_pgnn_kernel(tc, x, dist, w, b, offs, out):
         bias_8th = held.tile([FEATURES, 1], F32, name="bias_8th")
         nc.scalar.mul(bias_8th[:], bias[:], 1.0 / ANCHORS)
 
+        identity = held.tile([FEATURES, FEATURES], F32, name="identity")
+        make_identity(nc, identity[:])
+
         for half, anchor in pieces:
             first = anchor * NODES + half * PIECE
             own_columns = nodes_bf[:, half * PIECE : (half + 1) * PIECE]
@@ -64,12 +70,19 @@ def tile_pgnn_kernel(tc, x, dist, w, b, offs, out):
             nc.tensor.matmul(pre[:], w_own[:], own_columns, start=True, stop=False)
             nc.tensor.matmul(pre[:], w_msg[:], message[:], start=False, stop=True)
 
+            hidden = ring.tile([FEATURES, PIECE], F32, name="hidden")
+            nc.scalar.activation(hidden[:], pre[:], RELU, bias=bias_8th[:], scale=1.0 / ANCHORS)
+
             if anchor == 0:
+                partial = sums.tile([FEATURES, PIECE], F32, name="partial")
+            if anchor < SUMMED_BY_TENSOR:
+                nc.tensor.matmul(
+                    partial[:], identity[:], hidden[:], start=anchor == 0, stop=anchor == SUMMED_BY_TENSOR - 1
+                )
+            elif anchor == SUMMED_BY_TENSOR:
                 mean = ring.tile([FEATURES, PIECE], F32, name="mean")
-                nc.scalar.activation(mean[:], pre[:], RELU, bias=bias_8th[:], scale=1.0 / ANCHORS)
+                nc.vector.tensor_tensor(mean[:], hidden[:], partial[:], ADD)
             else:
-                hidden = ring.tile([FEATURES, PIECE], F32, name="hidden")
-                nc.scalar.activation(hidden[:], pre[:], RELU, bias=bias_8th[:], scale=1.0 / ANCHORS)
                 nc.vector.tensor_tensor(mean[:], mean[:], hidden[:], ADD)
             if anchor == ANCHORS - 1:
                 nc.sync.dma_start(out[:, half * PIECE : (half + 1) * PIECE], mean[:])

@@ -1,5 +1,4 @@
 import concourse.mybir as mybir
-from concourse.masks import make_identity
 
 F32 = mybir.dt.float32
 BF16 = mybir.dt.bfloat16
@@ -15,7 +14,6 @@ ANCHORS = 8
 PIECE = 512
 HALVES = NODES // PIECE
 ENTRIES = ANCHORS * NODES
-SUMMED_BY_TENSOR = 6
 
 FLOPS = 2 * FEATURES * FEATURES * (ENTRIES + NODES)
 
@@ -26,7 +24,6 @@ def tile_pgnn_kernel(tc, x, dist, w, b, offs, out):
         tc.tile_pool(name="held", bufs=1) as held,
         tc.tile_pool(name="ring", bufs=4) as ring,
         tc.psum_pool(name="psum", bufs=4) as psum,
-        tc.psum_pool(name="sums", bufs=HALVES) as sums,
     ):
         offsets = held.tile([FEATURES, ENTRIES // 16], U16, name="offsets")
         nc.sync.dma_start(offsets[:], offs)
@@ -52,9 +49,6 @@ def tile_pgnn_kernel(tc, x, dist, w, b, offs, out):
         bias_8th = held.tile([FEATURES, 1], F32, name="bias_8th")
         nc.scalar.mul(bias_8th[:], bias[:], 1.0 / ANCHORS)
 
-        identity = held.tile([FEATURES, FEATURES], F32, name="identity")
-        make_identity(nc, identity[:])
-
         for half, anchor in pieces:
             first = anchor * NODES + half * PIECE
             own_columns = nodes_bf[:, half * PIECE : (half + 1) * PIECE]
@@ -70,19 +64,12 @@ def tile_pgnn_kernel(tc, x, dist, w, b, offs, out):
             nc.tensor.matmul(pre[:], w_own[:], own_columns, start=True, stop=False)
             nc.tensor.matmul(pre[:], w_msg[:], message[:], start=False, stop=True)
 
-            hidden = ring.tile([FEATURES, PIECE], F32, name="hidden")
-            nc.scalar.activation(hidden[:], pre[:], RELU, bias=bias_8th[:], scale=1.0 / ANCHORS)
-
             if anchor == 0:
-                partial = sums.tile([FEATURES, PIECE], F32, name="partial")
-            if anchor < SUMMED_BY_TENSOR:
-                nc.tensor.matmul(
-                    partial[:], identity[:], hidden[:], start=anchor == 0, stop=anchor == SUMMED_BY_TENSOR - 1
-                )
-            elif anchor == SUMMED_BY_TENSOR:
                 mean = ring.tile([FEATURES, PIECE], F32, name="mean")
-                nc.vector.tensor_tensor(mean[:], hidden[:], partial[:], ADD)
+                nc.scalar.activation(mean[:], pre[:], RELU, bias=bias_8th[:], scale=1.0 / ANCHORS)
             else:
-                nc.vector.tensor_tensor(mean[:], mean[:], hidden[:], ADD)
+                hidden = ring.tile([FEATURES, PIECE], F32, name="hidden")
+                nc.scalar.activation(hidden[:], pre[:], RELU, bias=bias_8th[:], scale=1.0 / ANCHORS)
+                nc.gpsimd.tensor_tensor(mean[:], mean[:], hidden[:], ADD)
             if anchor == ANCHORS - 1:
                 nc.sync.dma_start(out[:, half * PIECE : (half + 1) * PIECE], mean[:])

@@ -1,10 +1,12 @@
 import concourse.mybir as mybir
+from concourse.masks import make_identity
 
 F32 = mybir.dt.float32
 BF16 = mybir.dt.bfloat16
 U16 = mybir.dt.uint16
 MULT = mybir.AluOpType.mult
 ADD = mybir.AluOpType.add
+MAX = mybir.AluOpType.max
 COPY = mybir.ActivationFunctionType.Copy
 RELU = mybir.ActivationFunctionType.Relu
 
@@ -14,6 +16,8 @@ ANCHORS = 8
 PIECE = 512
 HALVES = NODES // PIECE
 ENTRIES = ANCHORS * NODES
+SUMMED_BY_TENSOR = 5
+SUMMED_BY_VECTOR = ANCHORS - SUMMED_BY_TENSOR
 
 FLOPS = 2 * FEATURES * FEATURES * (ENTRIES + NODES)
 
@@ -22,8 +26,12 @@ def tile_pgnn_kernel(tc, x, dist, w, b, offs, out):
     nc = tc.nc
     with (
         tc.tile_pool(name="held", bufs=1) as held,
-        tc.tile_pool(name="ring", bufs=4) as ring,
-        tc.psum_pool(name="psum", bufs=4) as psum,
+        tc.tile_pool(name="weighted", bufs=4) as weighted_ring,
+        tc.tile_pool(name="message", bufs=3) as message_ring,
+        tc.tile_pool(name="hidden", bufs=4) as hidden_ring,
+        tc.tile_pool(name="mean", bufs=HALVES) as mean_ring,
+        tc.psum_pool(name="psum", bufs=6) as psum,
+        tc.psum_pool(name="sums", bufs=HALVES) as sums,
     ):
         offsets = held.tile([FEATURES, ENTRIES // 16], U16, name="offsets")
         nc.sync.dma_start(offsets[:], offs)
@@ -46,30 +54,49 @@ def tile_pgnn_kernel(tc, x, dist, w, b, offs, out):
 
         nodes_bf = held.tile([FEATURES, NODES], BF16, name="nodes_bf")
         nc.scalar.activation(nodes_bf[:], nodes[:], COPY)
+
+        w_msg_8th = held.tile([FEATURES, FEATURES], BF16, name="w_msg_8th")
+        nc.scalar.mul(w_msg_8th[:], w_msg[:], 1.0 / ANCHORS)
+        w_own_8th = held.tile([FEATURES, FEATURES], BF16, name="w_own_8th")
+        nc.scalar.mul(w_own_8th[:], w_own[:], 1.0 / ANCHORS)
         bias_8th = held.tile([FEATURES, 1], F32, name="bias_8th")
         nc.scalar.mul(bias_8th[:], bias[:], 1.0 / ANCHORS)
+        minus_bias_8th = held.tile([FEATURES, 1], F32, name="minus_bias_8th")
+        nc.scalar.mul(minus_bias_8th[:], bias[:], -1.0 / ANCHORS)
+        bias_owed = held.tile([FEATURES, 1], F32, name="bias_owed")
+        nc.scalar.mul(bias_owed[:], bias[:], (SUMMED_BY_VECTOR - 1.0) / ANCHORS)
+
+        identity = held.tile([FEATURES, FEATURES], F32, name="identity")
+        make_identity(nc, identity[:])
 
         for half, anchor in pieces:
             first = anchor * NODES + half * PIECE
             own_columns = nodes_bf[:, half * PIECE : (half + 1) * PIECE]
 
             picked = nodes[:].indirect(offsets[:, first // 16 : (first + PIECE) // 16])
-            weighted = ring.tile([FEATURES, PIECE], F32, name="weighted")
+            weighted = weighted_ring.tile([FEATURES, PIECE], F32, name="weighted")
             nc.vector.tensor_tensor(weighted[:], picked, scores[half, anchor][:], MULT)
 
-            message = ring.tile([FEATURES, PIECE], BF16, name="message")
+            message = message_ring.tile([FEATURES, PIECE], BF16, name="message")
             nc.scalar.activation(message[:], weighted[:], COPY)
 
             pre = psum.tile([FEATURES, PIECE], F32, name="pre")
-            nc.tensor.matmul(pre[:], w_own[:], own_columns, start=True, stop=False)
-            nc.tensor.matmul(pre[:], w_msg[:], message[:], start=False, stop=True)
+            nc.tensor.matmul(pre[:], w_own_8th[:], own_columns, start=True, stop=False)
+            nc.tensor.matmul(pre[:], w_msg_8th[:], message[:], start=False, stop=True)
 
-            if anchor == 0:
-                mean = ring.tile([FEATURES, PIECE], F32, name="mean")
-                nc.scalar.activation(mean[:], pre[:], RELU, bias=bias_8th[:], scale=1.0 / ANCHORS)
+            if anchor < SUMMED_BY_TENSOR:
+                hidden = hidden_ring.tile([FEATURES, PIECE], F32, name="hidden")
+                nc.scalar.activation(hidden[:], pre[:], RELU, bias=bias_8th[:])
+                if anchor == 0:
+                    partial = sums.tile([FEATURES, PIECE], F32, name="partial")
+                nc.tensor.matmul(
+                    partial[:], identity[:], hidden[:], start=anchor == 0, stop=anchor == SUMMED_BY_TENSOR - 1
+                )
+            elif anchor == SUMMED_BY_TENSOR:
+                mean = mean_ring.tile([FEATURES, PIECE], F32, name="mean")
+                nc.scalar.activation(mean[:], pre[:], RELU, bias=bias_8th[:])
+                nc.vector.scalar_tensor_tensor(mean[:], mean[:], bias_owed[:], partial[:], ADD, ADD)
             else:
-                hidden = ring.tile([FEATURES, PIECE], F32, name="hidden")
-                nc.scalar.activation(hidden[:], pre[:], RELU, bias=bias_8th[:], scale=1.0 / ANCHORS)
-                nc.gpsimd.tensor_tensor(mean[:], mean[:], hidden[:], ADD)
+                nc.vector.scalar_tensor_tensor(mean[:], pre[:], minus_bias_8th[:], mean[:], MAX, ADD)
             if anchor == ANCHORS - 1:
                 nc.sync.dma_start(out[:, half * PIECE : (half + 1) * PIECE], mean[:])

@@ -16,8 +16,11 @@ ANCHORS = 8
 PIECE = 512
 HALVES = NODES // PIECE
 ENTRIES = ANCHORS * NODES
+BLOCK = 128
+BLOCKS = PIECE // BLOCK
 SUMMED_BY_TENSOR = 5
 SUMMED_BY_VECTOR = ANCHORS - SUMMED_BY_TENSOR
+PRE_BANKS = 8 - HALVES
 
 FLOPS = 2 * FEATURES * FEATURES * (ENTRIES + NODES)
 
@@ -26,11 +29,8 @@ def tile_pgnn_kernel(tc, x, dist, w, b, offs, out):
     nc = tc.nc
     with (
         tc.tile_pool(name="held", bufs=1) as held,
-        tc.tile_pool(name="weighted", bufs=4) as weighted_ring,
-        tc.tile_pool(name="message", bufs=3) as message_ring,
         tc.tile_pool(name="hidden", bufs=4) as hidden_ring,
-        tc.tile_pool(name="mean", bufs=HALVES) as mean_ring,
-        tc.psum_pool(name="psum", bufs=6) as psum,
+        tc.psum_pool(name="psum", bufs=PRE_BANKS) as psum,
         tc.psum_pool(name="sums", bufs=HALVES) as sums,
     ):
         offsets = held.tile([FEATURES, ENTRIES // 16], U16, name="offsets")
@@ -44,13 +44,13 @@ def tile_pgnn_kernel(tc, x, dist, w, b, offs, out):
         bias = held.tile([FEATURES, 1], F32, name="bias")
         nc.scalar.dma_start(bias[:], b)
 
-        pieces = [(half, anchor) for half in range(HALVES) for anchor in range(ANCHORS)]
+        pieces = [(anchor, half) for anchor in range(ANCHORS) for half in range(HALVES)]
 
         scores = {}
-        for half, anchor in pieces:
+        for anchor, half in pieces:
             first = anchor * NODES + half * PIECE
-            scores[half, anchor] = held.tile([FEATURES, PIECE], F32, name=f"scores_{half}_{anchor}")
-            nc.sync.dma_start(scores[half, anchor][:], dist[:, first : first + PIECE])
+            scores[anchor, half] = held.tile([FEATURES, PIECE], F32, name=f"scores_{anchor}_{half}")
+            nc.sync.dma_start(scores[anchor, half][:], dist[:, first : first + PIECE])
 
         nodes_bf = held.tile([FEATURES, NODES], BF16, name="nodes_bf")
         nc.scalar.activation(nodes_bf[:], nodes[:], COPY)
@@ -69,34 +69,68 @@ def tile_pgnn_kernel(tc, x, dist, w, b, offs, out):
         identity = held.tile([FEATURES, FEATURES], F32, name="identity")
         make_identity(nc, identity[:])
 
-        for half, anchor in pieces:
+        weighted = {}
+        message = {}
+        pre = {}
+        flipped_sum = [sums.tile([BLOCK, BLOCKS * FEATURES], F32, name=f"flipped_sum_{half}", tag="sum") for half in range(HALVES)]
+        partial = {}
+        mean = [held.tile([FEATURES, PIECE], F32, name=f"mean_{half}") for half in range(HALVES)]
+
+        def look_up(anchor, half):
             first = anchor * NODES + half * PIECE
-            own_columns = nodes_bf[:, half * PIECE : (half + 1) * PIECE]
-
             picked = nodes[:].indirect(offsets[:, first // 16 : (first + PIECE) // 16])
-            weighted = weighted_ring.tile([FEATURES, PIECE], F32, name="weighted")
-            nc.vector.tensor_tensor(weighted[:], picked, scores[half, anchor][:], MULT)
+            weighted[anchor, half] = held.tile([FEATURES, PIECE], F32, name=f"weighted_{anchor}_{half}")
+            nc.vector.tensor_tensor(weighted[anchor, half][:], picked, scores[anchor, half][:], MULT)
 
-            message = message_ring.tile([FEATURES, PIECE], BF16, name="message")
-            nc.scalar.activation(message[:], weighted[:], COPY)
+        def project(anchor, half):
+            message[anchor, half] = held.tile([FEATURES, PIECE], BF16, name=f"message_{anchor}_{half}")
+            nc.scalar.activation(message[anchor, half][:], weighted[anchor, half][:], COPY)
+            pre[anchor, half] = psum.tile([FEATURES, PIECE], F32, name="pre")
+            own_columns = nodes_bf[:, half * PIECE : (half + 1) * PIECE]
+            nc.tensor.matmul(pre[anchor, half][:], w_own_8th[:], own_columns, start=True, stop=False)
+            nc.tensor.matmul(pre[anchor, half][:], w_msg_8th[:], message[anchor, half][:], start=False, stop=True)
 
-            pre = psum.tile([FEATURES, PIECE], F32, name="pre")
-            nc.tensor.matmul(pre[:], w_own_8th[:], own_columns, start=True, stop=False)
-            nc.tensor.matmul(pre[:], w_msg_8th[:], message[:], start=False, stop=True)
-
+        def rectify_on_scalar(anchor, half):
             if anchor < SUMMED_BY_TENSOR:
                 hidden = hidden_ring.tile([FEATURES, PIECE], F32, name="hidden")
-                nc.scalar.activation(hidden[:], pre[:], RELU, bias=bias_8th[:])
-                if anchor == 0:
-                    partial = sums.tile([FEATURES, PIECE], F32, name="partial")
-                nc.tensor.matmul(
-                    partial[:], identity[:], hidden[:], start=anchor == 0, stop=anchor == SUMMED_BY_TENSOR - 1
-                )
+                nc.scalar.activation(hidden[:], pre[anchor, half][:], RELU, bias=bias_8th[:])
+                for block in range(BLOCKS):
+                    nc.tensor.matmul(
+                        flipped_sum[half][:, block * FEATURES : (block + 1) * FEATURES],
+                        hidden[:, block * BLOCK : (block + 1) * BLOCK],
+                        identity[:],
+                        is_transpose=True,
+                        start=anchor == 0 and block == 0,
+                        stop=anchor == SUMMED_BY_TENSOR - 1 and block == BLOCKS - 1,
+                    )
+                if anchor == SUMMED_BY_TENSOR - 1:
+                    flipped = held.tile([BLOCK, BLOCKS * FEATURES], F32, name=f"flipped_{half}")
+                    nc.scalar.activation(flipped[:], flipped_sum[half][:], COPY)
+                    partial[half] = sums.tile([FEATURES, PIECE], F32, name=f"partial_{half}", tag="sum")
+                    for block in range(BLOCKS):
+                        nc.tensor.transpose(
+                            partial[half][:, block * BLOCK : (block + 1) * BLOCK],
+                            flipped[:, block * FEATURES : (block + 1) * FEATURES],
+                            identity[:],
+                        )
             elif anchor == SUMMED_BY_TENSOR:
-                mean = mean_ring.tile([FEATURES, PIECE], F32, name="mean")
-                nc.scalar.activation(mean[:], pre[:], RELU, bias=bias_8th[:])
-                nc.vector.scalar_tensor_tensor(mean[:], mean[:], bias_owed[:], partial[:], ADD, ADD)
-            else:
-                nc.vector.scalar_tensor_tensor(mean[:], pre[:], minus_bias_8th[:], mean[:], MAX, ADD)
-            if anchor == ANCHORS - 1:
-                nc.sync.dma_start(out[:, half * PIECE : (half + 1) * PIECE], mean[:])
+                nc.scalar.activation(mean[half][:], pre[anchor, half][:], RELU, bias=bias_8th[:])
+
+        for step in range(len(pieces) + 2):
+            if step < len(pieces):
+                look_up(*pieces[step])
+            if 1 <= step <= len(pieces):
+                project(*pieces[step - 1])
+            if step >= 2:
+                rectify_on_scalar(*pieces[step - 2])
+
+        for anchor in range(SUMMED_BY_TENSOR + 1, ANCHORS):
+            for half in range(HALVES):
+                nc.vector.scalar_tensor_tensor(
+                    mean[half][:], pre[anchor, half][:], minus_bias_8th[:], mean[half][:], MAX, ADD
+                )
+            if anchor == SUMMED_BY_TENSOR + 1:
+                for half in range(HALVES):
+                    nc.vector.scalar_tensor_tensor(mean[half][:], mean[half][:], bias_owed[:], partial[half][:], ADD, ADD)
+        for half in range(HALVES):
+            nc.sync.dma_start(out[:, half * PIECE : (half + 1) * PIECE], mean[half][:])

@@ -18,7 +18,7 @@ HALVES = NODES // PIECE
 ENTRIES = ANCHORS * NODES
 BLOCK = 128
 BLOCKS = PIECE // BLOCK
-SUMMED_BY_TENSOR = 5
+SUMMED_BY_TENSOR = 6
 SUMMED_BY_VECTOR = ANCHORS - SUMMED_BY_TENSOR
 PRE_BANKS = 8 - HALVES
 
@@ -84,7 +84,10 @@ def tile_pgnn_kernel(tc, x, dist, w, b, offs, out):
 
         def project(anchor, half):
             message[anchor, half] = held.tile([FEATURES, PIECE], BF16, name=f"message_{anchor}_{half}")
-            nc.scalar.activation(message[anchor, half][:], weighted[anchor, half][:], COPY)
+            if anchor < ANCHORS - 1:
+                nc.scalar.activation(message[anchor, half][:], weighted[anchor, half][:], COPY)
+            else:
+                nc.vector.tensor_copy(message[anchor, half][:], weighted[anchor, half][:])
             pre[anchor, half] = psum.tile([FEATURES, PIECE], F32, name="pre")
             own_columns = nodes_bf[:, half * PIECE : (half + 1) * PIECE]
             nc.tensor.matmul(pre[anchor, half][:], w_own_8th[:], own_columns, start=True, stop=False)
@@ -124,13 +127,12 @@ def tile_pgnn_kernel(tc, x, dist, w, b, offs, out):
             if step >= 2:
                 rectify_on_scalar(*pieces[step - 2])
 
+        for half in range(HALVES):
+            nc.vector.scalar_tensor_tensor(mean[half][:], mean[half][:], bias_owed[:], partial[half][:], ADD, ADD)
         for anchor in range(SUMMED_BY_TENSOR + 1, ANCHORS):
             for half in range(HALVES):
                 nc.vector.scalar_tensor_tensor(
                     mean[half][:], pre[anchor, half][:], minus_bias_8th[:], mean[half][:], MAX, ADD
                 )
-            if anchor == SUMMED_BY_TENSOR + 1:
-                for half in range(HALVES):
-                    nc.vector.scalar_tensor_tensor(mean[half][:], mean[half][:], bias_owed[:], partial[half][:], ADD, ADD)
         for half in range(HALVES):
             nc.sync.dma_start(out[:, half * PIECE : (half + 1) * PIECE], mean[half][:])

@@ -20,6 +20,7 @@ BLOCK = 128
 BLOCKS = PIECE // BLOCK
 SUMMED_BY_TENSOR = 6
 SUMMED_BY_VECTOR = ANCHORS - SUMMED_BY_TENSOR
+FIRST_CUT = PIECE // 4
 PRE_BANKS = 8 - HALVES
 
 FLOPS = 2 * FEATURES * FEATURES * (ENTRIES + NODES)
@@ -33,38 +34,44 @@ def tile_pgnn_kernel(tc, x, dist, w, b, offs, out):
         tc.psum_pool(name="psum", bufs=PRE_BANKS) as psum,
         tc.psum_pool(name="sums", bufs=HALVES) as sums,
     ):
+        w_msg = held.tile([FEATURES, FEATURES], BF16, name="w_msg")
+        nc.sync.dma_start(w_msg[:], w[0:FEATURES, :])
+        w_own = held.tile([FEATURES, FEATURES], BF16, name="w_own")
+        nc.sync.dma_start(w_own[:], w[FEATURES : 2 * FEATURES, :])
+        bias = held.tile([FEATURES, 1], F32, name="bias")
+        nc.sync.dma_start(bias[:], b)
         offsets = held.tile([FEATURES, ENTRIES // 16], U16, name="offsets")
         nc.sync.dma_start(offsets[:], offs)
         nodes = held.tile([FEATURES, NODES], F32, name="nodes")
         nc.scalar.dma_start(nodes[:], x)
-        w_msg = held.tile([FEATURES, FEATURES], BF16, name="w_msg")
-        nc.scalar.dma_start(w_msg[:], w[0:FEATURES, :])
-        w_own = held.tile([FEATURES, FEATURES], BF16, name="w_own")
-        nc.scalar.dma_start(w_own[:], w[FEATURES : 2 * FEATURES, :])
-        bias = held.tile([FEATURES, 1], F32, name="bias")
-        nc.scalar.dma_start(bias[:], b)
 
         pieces = [(anchor, half) for anchor in range(ANCHORS) for half in range(HALVES)]
+
+        def cuts(anchor, half):
+            if (anchor, half) == pieces[0]:
+                return ((0, FIRST_CUT), (FIRST_CUT, PIECE))
+            return ((0, PIECE),)
 
         scores = {}
         for anchor, half in pieces:
             first = anchor * NODES + half * PIECE
             scores[anchor, half] = held.tile([FEATURES, PIECE], F32, name=f"scores_{anchor}_{half}")
-            nc.sync.dma_start(scores[anchor, half][:], dist[:, first : first + PIECE])
+            for low, high in cuts(anchor, half):
+                nc.sync.dma_start(scores[anchor, half][:, low:high], dist[:, first + low : first + high])
 
         nodes_bf = held.tile([FEATURES, NODES], BF16, name="nodes_bf")
         nc.scalar.activation(nodes_bf[:], nodes[:], COPY)
 
         w_msg_8th = held.tile([FEATURES, FEATURES], BF16, name="w_msg_8th")
-        nc.scalar.mul(w_msg_8th[:], w_msg[:], 1.0 / ANCHORS)
+        nc.vector.tensor_scalar_mul(w_msg_8th[:], w_msg[:], 1.0 / ANCHORS)
         w_own_8th = held.tile([FEATURES, FEATURES], BF16, name="w_own_8th")
-        nc.scalar.mul(w_own_8th[:], w_own[:], 1.0 / ANCHORS)
+        nc.vector.tensor_scalar_mul(w_own_8th[:], w_own[:], 1.0 / ANCHORS)
         bias_8th = held.tile([FEATURES, 1], F32, name="bias_8th")
-        nc.scalar.mul(bias_8th[:], bias[:], 1.0 / ANCHORS)
+        nc.vector.tensor_scalar_mul(bias_8th[:], bias[:], 1.0 / ANCHORS)
         minus_bias_8th = held.tile([FEATURES, 1], F32, name="minus_bias_8th")
-        nc.scalar.mul(minus_bias_8th[:], bias[:], -1.0 / ANCHORS)
+        nc.vector.tensor_scalar_mul(minus_bias_8th[:], bias[:], -1.0 / ANCHORS)
         bias_owed = held.tile([FEATURES, 1], F32, name="bias_owed")
-        nc.scalar.mul(bias_owed[:], bias[:], (SUMMED_BY_VECTOR - 1.0) / ANCHORS)
+        nc.vector.tensor_scalar_mul(bias_owed[:], bias[:], (SUMMED_BY_VECTOR - 1.0) / ANCHORS)
 
         identity = held.tile([FEATURES, FEATURES], F32, name="identity")
         make_identity(nc, identity[:])
@@ -78,9 +85,10 @@ def tile_pgnn_kernel(tc, x, dist, w, b, offs, out):
 
         def look_up(anchor, half):
             first = anchor * NODES + half * PIECE
-            picked = nodes[:].indirect(offsets[:, first // 16 : (first + PIECE) // 16])
             weighted[anchor, half] = held.tile([FEATURES, PIECE], F32, name=f"weighted_{anchor}_{half}")
-            nc.vector.tensor_tensor(weighted[anchor, half][:], picked, scores[anchor, half][:], MULT)
+            for low, high in cuts(anchor, half):
+                picked = nodes[:].indirect(offsets[:, (first + low) // 16 : (first + high) // 16])
+                nc.vector.tensor_tensor(weighted[anchor, half][:, low:high], picked, scores[anchor, half][:, low:high], MULT)
 
         def project(anchor, half):
             message[anchor, half] = held.tile([FEATURES, PIECE], BF16, name=f"message_{anchor}_{half}")

@@ -34,12 +34,6 @@ def tile_pgnn_kernel(tc, x, dist, w, b, offs, out):
         tc.psum_pool(name="psum", bufs=PRE_BANKS) as psum,
         tc.psum_pool(name="sums", bufs=HALVES) as sums,
     ):
-        w_msg = held.tile([FEATURES, FEATURES], BF16, name="w_msg")
-        nc.sync.dma_start(w_msg[:], w[0:FEATURES, :])
-        w_own = held.tile([FEATURES, FEATURES], BF16, name="w_own")
-        nc.sync.dma_start(w_own[:], w[FEATURES : 2 * FEATURES, :])
-        bias = held.tile([FEATURES, 1], F32, name="bias")
-        nc.sync.dma_start(bias[:], b)
         offsets = held.tile([FEATURES, ENTRIES // 16], U16, name="offsets")
         nc.sync.dma_start(offsets[:], offs)
         nodes = held.tile([FEATURES, NODES], F32, name="nodes")
@@ -58,20 +52,22 @@ def tile_pgnn_kernel(tc, x, dist, w, b, offs, out):
             scores[anchor, half] = held.tile([FEATURES, PIECE], F32, name=f"scores_{anchor}_{half}")
             for low, high in cuts(anchor, half):
                 nc.sync.dma_start(scores[anchor, half][:, low:high], dist[:, first + low : first + high])
+            if (anchor, half) == pieces[0]:
+                w_own = held.tile([FEATURES, FEATURES], BF16, name="w_own")
+                nc.sync.dma_start(w_own[:], w[FEATURES : 2 * FEATURES, :])
+                w_msg = held.tile([FEATURES, FEATURES], BF16, name="w_msg")
+                nc.sync.dma_start(w_msg[:], w[0:FEATURES, :])
+                bias = held.tile([FEATURES, 1], F32, name="bias")
+                nc.sync.dma_start(bias[:], b)
 
         nodes_bf = held.tile([FEATURES, NODES], BF16, name="nodes_bf")
-        nc.scalar.activation(nodes_bf[:], nodes[:], COPY)
-
-        w_msg_8th = held.tile([FEATURES, FEATURES], BF16, name="w_msg_8th")
-        nc.vector.tensor_scalar_mul(w_msg_8th[:], w_msg[:], 1.0 / ANCHORS)
-        w_own_8th = held.tile([FEATURES, FEATURES], BF16, name="w_own_8th")
-        nc.vector.tensor_scalar_mul(w_own_8th[:], w_own[:], 1.0 / ANCHORS)
+        nc.scalar.activation(nodes_bf[:], nodes[:], COPY, scale=1.0 / ANCHORS)
         bias_8th = held.tile([FEATURES, 1], F32, name="bias_8th")
-        nc.vector.tensor_scalar_mul(bias_8th[:], bias[:], 1.0 / ANCHORS)
+        nc.scalar.mul(bias_8th[:], bias[:], 1.0 / ANCHORS)
         minus_bias_8th = held.tile([FEATURES, 1], F32, name="minus_bias_8th")
-        nc.vector.tensor_scalar_mul(minus_bias_8th[:], bias[:], -1.0 / ANCHORS)
+        nc.scalar.mul(minus_bias_8th[:], bias[:], -1.0 / ANCHORS)
         bias_owed = held.tile([FEATURES, 1], F32, name="bias_owed")
-        nc.vector.tensor_scalar_mul(bias_owed[:], bias[:], (SUMMED_BY_VECTOR - 1.0) / ANCHORS)
+        nc.scalar.mul(bias_owed[:], bias[:], (SUMMED_BY_VECTOR - 1.0) / ANCHORS)
 
         identity = held.tile([FEATURES, FEATURES], F32, name="identity")
         make_identity(nc, identity[:])
@@ -93,13 +89,13 @@ def tile_pgnn_kernel(tc, x, dist, w, b, offs, out):
         def project(anchor, half):
             message[anchor, half] = held.tile([FEATURES, PIECE], BF16, name=f"message_{anchor}_{half}")
             if anchor < ANCHORS - 1:
-                nc.scalar.activation(message[anchor, half][:], weighted[anchor, half][:], COPY)
+                nc.scalar.activation(message[anchor, half][:], weighted[anchor, half][:], COPY, scale=1.0 / ANCHORS)
             else:
-                nc.vector.tensor_copy(message[anchor, half][:], weighted[anchor, half][:])
+                nc.vector.tensor_scalar_mul(message[anchor, half][:], weighted[anchor, half][:], 1.0 / ANCHORS)
             pre[anchor, half] = psum.tile([FEATURES, PIECE], F32, name="pre")
             own_columns = nodes_bf[:, half * PIECE : (half + 1) * PIECE]
-            nc.tensor.matmul(pre[anchor, half][:], w_own_8th[:], own_columns, start=True, stop=False)
-            nc.tensor.matmul(pre[anchor, half][:], w_msg_8th[:], message[anchor, half][:], start=False, stop=True)
+            nc.tensor.matmul(pre[anchor, half][:], w_own[:], own_columns, start=True, stop=False)
+            nc.tensor.matmul(pre[anchor, half][:], w_msg[:], message[anchor, half][:], start=False, stop=True)
 
         def rectify_on_scalar(anchor, half):
             if anchor < SUMMED_BY_TENSOR:

@@ -20,7 +20,6 @@ BLOCK = 128
 BLOCKS = PIECE // BLOCK
 SUMMED_BY_TENSOR = 6
 SUMMED_BY_VECTOR = ANCHORS - SUMMED_BY_TENSOR
-FIRST_CUT = PIECE // 4
 PRE_BANKS = 8 - HALVES
 
 FLOPS = 2 * FEATURES * FEATURES * (ENTRIES + NODES)
@@ -41,17 +40,11 @@ def tile_pgnn_kernel(tc, x, dist, w, b, offs, out):
 
         pieces = [(anchor, half) for anchor in range(ANCHORS) for half in range(HALVES)]
 
-        def cuts(anchor, half):
-            if (anchor, half) == pieces[0]:
-                return ((0, FIRST_CUT), (FIRST_CUT, PIECE))
-            return ((0, PIECE),)
-
         scores = {}
         for anchor, half in pieces:
             first = anchor * NODES + half * PIECE
             scores[anchor, half] = held.tile([FEATURES, PIECE], F32, name=f"scores_{anchor}_{half}")
-            for low, high in cuts(anchor, half):
-                nc.sync.dma_start(scores[anchor, half][:, low:high], dist[:, first + low : first + high])
+            nc.sync.dma_start(scores[anchor, half][:], dist[:, first : first + PIECE])
             if (anchor, half) == pieces[0]:
                 w_own = held.tile([FEATURES, FEATURES], BF16, name="w_own")
                 nc.sync.dma_start(w_own[:], w[FEATURES : 2 * FEATURES, :])
@@ -82,9 +75,8 @@ def tile_pgnn_kernel(tc, x, dist, w, b, offs, out):
         def look_up(anchor, half):
             first = anchor * NODES + half * PIECE
             weighted[anchor, half] = held.tile([FEATURES, PIECE], F32, name=f"weighted_{anchor}_{half}")
-            for low, high in cuts(anchor, half):
-                picked = nodes[:].indirect(offsets[:, (first + low) // 16 : (first + high) // 16])
-                nc.vector.tensor_tensor(weighted[anchor, half][:, low:high], picked, scores[anchor, half][:, low:high], MULT)
+            picked = nodes[:].indirect(offsets[:, first // 16 : (first + PIECE) // 16])
+            nc.vector.tensor_tensor(weighted[anchor, half][:], picked, scores[anchor, half][:], MULT)
 
         def project(anchor, half):
             message[anchor, half] = held.tile([FEATURES, PIECE], BF16, name=f"message_{anchor}_{half}")

@@ -13,16 +13,22 @@ RELU = mybir.ActivationFunctionType.Relu
 FEATURES = 128
 NODES = 1024
 ANCHORS = 8
-PIECE = 512
-HALVES = NODES // PIECE
+BANK = 512
+HALVES = NODES // BANK
 ENTRIES = ANCHORS * NODES
 BLOCK = 128
-BLOCKS = PIECE // BLOCK
+BLOCKS = BANK // BLOCK
 SUMMED_BY_TENSOR = 6
 SUMMED_BY_VECTOR = ANCHORS - SUMMED_BY_TENSOR
 PRE_BANKS = 8 - HALVES
 
 FLOPS = 2 * FEATURES * FEATURES * (ENTRIES + NODES)
+
+
+def cuts_of(anchor):
+    if anchor == 0:
+        return [(0, BLOCK), (BLOCK, BANK - BLOCK), (BANK, BANK)]
+    return [(0, BANK), (BANK, BANK)]
 
 
 def tile_pgnn_kernel(tc, x, dist, w, b, offs, out):
@@ -33,19 +39,22 @@ def tile_pgnn_kernel(tc, x, dist, w, b, offs, out):
         tc.psum_pool(name="psum", bufs=PRE_BANKS) as psum,
         tc.psum_pool(name="sums", bufs=HALVES) as sums,
     ):
+        pieces = [(anchor, start, width) for anchor in range(ANCHORS) for start, width in cuts_of(anchor)]
+
         offsets = held.tile([FEATURES, ENTRIES // 16], U16, name="offsets")
         nc.sync.dma_start(offsets[:], offs)
         nodes = held.tile([FEATURES, NODES], F32, name="nodes")
-        nc.scalar.dma_start(nodes[:], x)
-
-        pieces = [(anchor, half) for anchor in range(ANCHORS) for half in range(HALVES)]
+        nc.sync.dma_start(nodes[:, 0:BANK], x[:, 0:BANK])
+        nc.scalar.dma_start(nodes[:, BANK:NODES], x[:, BANK:NODES])
 
         scores = {}
-        for anchor, half in pieces:
-            first = anchor * NODES + half * PIECE
-            scores[anchor, half] = held.tile([FEATURES, PIECE], F32, name=f"scores_{anchor}_{half}")
-            nc.sync.dma_start(scores[anchor, half][:], dist[:, first : first + PIECE])
-            if (anchor, half) == pieces[0]:
+        for piece in pieces:
+            anchor, start, width = piece
+            first = anchor * NODES + start
+            scores[piece] = held.tile([FEATURES, width], F32, name=f"scores_{anchor}_{start}")
+            queue = nc.scalar if piece == pieces[0] else nc.sync
+            queue.dma_start(scores[piece][:], dist[:, first : first + width])
+            if piece == pieces[1]:
                 w_own = held.tile([FEATURES, FEATURES], BF16, name="w_own")
                 nc.sync.dma_start(w_own[:], w[FEATURES : 2 * FEATURES, :])
                 w_msg = held.tile([FEATURES, FEATURES], BF16, name="w_msg")
@@ -70,65 +79,68 @@ def tile_pgnn_kernel(tc, x, dist, w, b, offs, out):
         pre = {}
         flipped_sum = [sums.tile([BLOCK, BLOCKS * FEATURES], F32, name=f"flipped_sum_{half}", tag="sum") for half in range(HALVES)]
         partial = {}
-        mean = [held.tile([FEATURES, PIECE], F32, name=f"mean_{half}") for half in range(HALVES)]
+        mean = held.tile([FEATURES, NODES], F32, name="mean")
 
-        def look_up(anchor, half):
-            first = anchor * NODES + half * PIECE
-            weighted[anchor, half] = held.tile([FEATURES, PIECE], F32, name=f"weighted_{anchor}_{half}")
-            picked = nodes[:].indirect(offsets[:, first // 16 : (first + PIECE) // 16])
-            nc.vector.tensor_tensor(weighted[anchor, half][:], picked, scores[anchor, half][:], MULT)
+        def look_up(piece):
+            anchor, start, width = piece
+            first = anchor * NODES + start
+            weighted[piece] = held.tile([FEATURES, width], F32, name=f"weighted_{anchor}_{start}")
+            picked = nodes[:].indirect(offsets[:, first // 16 : (first + width) // 16])
+            nc.vector.tensor_tensor(weighted[piece][:], picked, scores[piece][:], MULT)
 
-        def project(anchor, half):
-            message[anchor, half] = held.tile([FEATURES, PIECE], BF16, name=f"message_{anchor}_{half}")
+        def project(piece):
+            anchor, start, width = piece
+            message[piece] = held.tile([FEATURES, width], BF16, name=f"message_{anchor}_{start}")
             if anchor < ANCHORS - 1:
-                nc.scalar.activation(message[anchor, half][:], weighted[anchor, half][:], COPY, scale=1.0 / ANCHORS)
+                nc.scalar.activation(message[piece][:], weighted[piece][:], COPY, scale=1.0 / ANCHORS)
             else:
-                nc.vector.tensor_scalar_mul(message[anchor, half][:], weighted[anchor, half][:], 1.0 / ANCHORS)
-            pre[anchor, half] = psum.tile([FEATURES, PIECE], F32, name="pre")
-            own_columns = nodes_bf[:, half * PIECE : (half + 1) * PIECE]
-            nc.tensor.matmul(pre[anchor, half][:], w_own[:], own_columns, start=True, stop=False)
-            nc.tensor.matmul(pre[anchor, half][:], w_msg[:], message[anchor, half][:], start=False, stop=True)
+                nc.vector.tensor_scalar_mul(message[piece][:], weighted[piece][:], 1.0 / ANCHORS)
+            pre[piece] = psum.tile([FEATURES, width], F32, name="pre")
+            nc.tensor.matmul(pre[piece][:], w_own[:], nodes_bf[:, start : start + width], start=True, stop=False)
+            nc.tensor.matmul(pre[piece][:], w_msg[:], message[piece][:], start=False, stop=True)
 
-        def rectify_on_scalar(anchor, half):
+        def rectify_on_scalar(piece):
+            anchor, start, width = piece
+            half = start // BANK
             if anchor < SUMMED_BY_TENSOR:
-                hidden = hidden_ring.tile([FEATURES, PIECE], F32, name="hidden")
-                nc.scalar.activation(hidden[:], pre[anchor, half][:], RELU, bias=bias_8th[:])
-                for block in range(BLOCKS):
+                hidden = hidden_ring.tile([FEATURES, width], F32, name="hidden")
+                nc.scalar.activation(hidden[:], pre[piece][:], RELU, bias=bias_8th[:])
+                for column in range(0, width, BLOCK):
+                    place = start - half * BANK + column
                     nc.tensor.matmul(
-                        flipped_sum[half][:, block * FEATURES : (block + 1) * FEATURES],
-                        hidden[:, block * BLOCK : (block + 1) * BLOCK],
+                        flipped_sum[half][:, place : place + BLOCK],
+                        hidden[:, column : column + BLOCK],
                         identity[:],
                         is_transpose=True,
-                        start=anchor == 0 and block == 0,
-                        stop=anchor == SUMMED_BY_TENSOR - 1 and block == BLOCKS - 1,
+                        start=anchor == 0 and place == 0,
+                        stop=anchor == SUMMED_BY_TENSOR - 1 and place == BANK - BLOCK,
                     )
-                if anchor == SUMMED_BY_TENSOR - 1:
+                if anchor == SUMMED_BY_TENSOR - 1 and start + width == (half + 1) * BANK:
                     flipped = held.tile([BLOCK, BLOCKS * FEATURES], F32, name=f"flipped_{half}")
                     nc.scalar.activation(flipped[:], flipped_sum[half][:], COPY)
-                    partial[half] = sums.tile([FEATURES, PIECE], F32, name=f"partial_{half}", tag="sum")
-                    for block in range(BLOCKS):
+                    partial[half] = sums.tile([FEATURES, BANK], F32, name=f"partial_{half}", tag="sum")
+                    for place in range(0, BANK, BLOCK):
                         nc.tensor.transpose(
-                            partial[half][:, block * BLOCK : (block + 1) * BLOCK],
-                            flipped[:, block * FEATURES : (block + 1) * FEATURES],
-                            identity[:],
+                            partial[half][:, place : place + BLOCK], flipped[:, place : place + BLOCK], identity[:]
                         )
             elif anchor == SUMMED_BY_TENSOR:
-                nc.scalar.activation(mean[half][:], pre[anchor, half][:], RELU, bias=bias_8th[:])
+                nc.scalar.activation(mean[:, start : start + width], pre[piece][:], RELU, bias=bias_8th[:])
 
         for step in range(len(pieces) + 2):
             if step < len(pieces):
-                look_up(*pieces[step])
+                look_up(pieces[step])
             if 1 <= step <= len(pieces):
-                project(*pieces[step - 1])
+                project(pieces[step - 1])
             if step >= 2:
-                rectify_on_scalar(*pieces[step - 2])
+                rectify_on_scalar(pieces[step - 2])
 
         for half in range(HALVES):
-            nc.vector.scalar_tensor_tensor(mean[half][:], mean[half][:], bias_owed[:], partial[half][:], ADD, ADD)
-        for anchor in range(SUMMED_BY_TENSOR + 1, ANCHORS):
-            for half in range(HALVES):
-                nc.vector.scalar_tensor_tensor(
-                    mean[half][:], pre[anchor, half][:], minus_bias_8th[:], mean[half][:], MAX, ADD
-                )
+            columns = mean[:, half * BANK : (half + 1) * BANK]
+            nc.vector.scalar_tensor_tensor(columns, columns, bias_owed[:], partial[half][:], ADD, ADD)
+        for piece in pieces:
+            anchor, start, width = piece
+            if anchor > SUMMED_BY_TENSOR:
+                columns = mean[:, start : start + width]
+                nc.vector.scalar_tensor_tensor(columns, pre[piece][:], minus_bias_8th[:], columns, MAX, ADD)
         for half in range(HALVES):
-            nc.sync.dma_start(out[:, half * PIECE : (half + 1) * PIECE], mean[half][:])
+            nc.sync.dma_start(out[:, half * BANK : (half + 1) * BANK], mean[:, half * BANK : (half + 1) * BANK])

import concourse.mybir as mybir
from concourse.masks import make_identity

F32 = mybir.dt.float32
BF16 = mybir.dt.bfloat16
U16 = mybir.dt.uint16
MULT = mybir.AluOpType.mult
ADD = mybir.AluOpType.add
MAX = mybir.AluOpType.max
COPY = mybir.ActivationFunctionType.Copy
RELU = mybir.ActivationFunctionType.Relu

FEATURES = 128
NODES = 1024
ANCHORS = 8
BANK = 512
HALVES = NODES // BANK
ENTRIES = ANCHORS * NODES
BLOCK = 128
BLOCKS = BANK // BLOCK
SUMMED_BY_TENSOR = 6
SUMMED_BY_VECTOR = ANCHORS - SUMMED_BY_TENSOR
PRE_BANKS = 8 - HALVES

FLOPS = 2 * FEATURES * FEATURES * (ENTRIES + NODES)


def cuts_of(anchor):
    if anchor == 0:
        return [(0, BLOCK), (BLOCK, BANK - BLOCK), (BANK, BANK)]
    return [(0, BANK), (BANK, BANK)]


def tile_pgnn_kernel(tc, x, dist, w, b, offs, out):
    nc = tc.nc
    with (
        tc.tile_pool(name="held", bufs=1) as held,
        tc.tile_pool(name="hidden", bufs=4) as hidden_ring,
        tc.psum_pool(name="psum", bufs=PRE_BANKS) as psum,
        tc.psum_pool(name="sums", bufs=HALVES) as sums,
    ):
        pieces = [(anchor, start, width) for anchor in range(ANCHORS) for start, width in cuts_of(anchor)]

        offsets = held.tile([FEATURES, ENTRIES // 16], U16, name="offsets")
        nc.sync.dma_start(offsets[:], offs)
        nodes = held.tile([FEATURES, NODES], F32, name="nodes")
        nc.sync.dma_start(nodes[:, 0:BANK], x[:, 0:BANK])
        nc.scalar.dma_start(nodes[:, BANK:NODES], x[:, BANK:NODES])

        scores = {}
        for piece in pieces:
            anchor, start, width = piece
            first = anchor * NODES + start
            scores[piece] = held.tile([FEATURES, width], F32, name=f"scores_{anchor}_{start}")
            queue = nc.scalar if piece == pieces[0] else nc.sync
            queue.dma_start(scores[piece][:], dist[:, first : first + width])
            if piece == pieces[1]:
                w_own = held.tile([FEATURES, FEATURES], BF16, name="w_own")
                nc.sync.dma_start(w_own[:], w[FEATURES : 2 * FEATURES, :])
                w_msg = held.tile([FEATURES, FEATURES], BF16, name="w_msg")
                nc.sync.dma_start(w_msg[:], w[0:FEATURES, :])
                bias = held.tile([FEATURES, 1], F32, name="bias")
                nc.sync.dma_start(bias[:], b)

        nodes_bf = held.tile([FEATURES, NODES], BF16, name="nodes_bf")
        nc.scalar.activation(nodes_bf[:], nodes[:], COPY, scale=1.0 / ANCHORS)
        bias_8th = held.tile([FEATURES, 1], F32, name="bias_8th")
        nc.scalar.mul(bias_8th[:], bias[:], 1.0 / ANCHORS)
        minus_bias_8th = held.tile([FEATURES, 1], F32, name="minus_bias_8th")
        nc.scalar.mul(minus_bias_8th[:], bias[:], -1.0 / ANCHORS)
        bias_owed = held.tile([FEATURES, 1], F32, name="bias_owed")
        nc.scalar.mul(bias_owed[:], bias[:], (SUMMED_BY_VECTOR - 1.0) / ANCHORS)

        identity = held.tile([FEATURES, FEATURES], F32, name="identity")
        make_identity(nc, identity[:])

        weighted = {}
        message = {}
        pre = {}
        flipped_sum = [sums.tile([BLOCK, BLOCKS * FEATURES], F32, name=f"flipped_sum_{half}", tag="sum") for half in range(HALVES)]
        partial = {}
        mean = held.tile([FEATURES, NODES], F32, name="mean")

        def look_up(piece):
            anchor, start, width = piece
            first = anchor * NODES + start
            weighted[piece] = held.tile([FEATURES, width], F32, name=f"weighted_{anchor}_{start}")
            picked = nodes[:].indirect(offsets[:, first // 16 : (first + width) // 16])
            nc.vector.tensor_tensor(weighted[piece][:], picked, scores[piece][:], MULT)

        def project(piece):
            anchor, start, width = piece
            message[piece] = held.tile([FEATURES, width], BF16, name=f"message_{anchor}_{start}")
            if anchor < ANCHORS - 1:
                nc.scalar.activation(message[piece][:], weighted[piece][:], COPY, scale=1.0 / ANCHORS)
            else:
                nc.vector.tensor_scalar_mul(message[piece][:], weighted[piece][:], 1.0 / ANCHORS)
            pre[piece] = psum.tile([FEATURES, width], F32, name="pre")
            nc.tensor.matmul(pre[piece][:], w_own[:], nodes_bf[:, start : start + width], start=True, stop=False)
            nc.tensor.matmul(pre[piece][:], w_msg[:], message[piece][:], start=False, stop=True)

        def rectify_on_scalar(piece):
            anchor, start, width = piece
            half = start // BANK
            if anchor < SUMMED_BY_TENSOR:
                hidden = hidden_ring.tile([FEATURES, width], F32, name="hidden")
                nc.scalar.activation(hidden[:], pre[piece][:], RELU, bias=bias_8th[:])
                for column in range(0, width, BLOCK):
                    place = start - half * BANK + column
                    nc.tensor.matmul(
                        flipped_sum[half][:, place : place + BLOCK],
                        hidden[:, column : column + BLOCK],
                        identity[:],
                        is_transpose=True,
                        start=anchor == 0 and place == 0,
                        stop=anchor == SUMMED_BY_TENSOR - 1 and place == BANK - BLOCK,
                    )
                if anchor == SUMMED_BY_TENSOR - 1 and start + width == (half + 1) * BANK:
                    flipped = held.tile([BLOCK, BLOCKS * FEATURES], F32, name=f"flipped_{half}")
                    nc.scalar.activation(flipped[:], flipped_sum[half][:], COPY)
                    partial[half] = sums.tile([FEATURES, BANK], F32, name=f"partial_{half}", tag="sum")
                    for place in range(0, BANK, BLOCK):
                        nc.tensor.transpose(
                            partial[half][:, place : place + BLOCK], flipped[:, place : place + BLOCK], identity[:]
                        )
            elif anchor == SUMMED_BY_TENSOR:
                nc.scalar.activation(mean[:, start : start + width], pre[piece][:], RELU, bias=bias_8th[:])

        for step in range(len(pieces) + 2):
            if step < len(pieces):
                look_up(pieces[step])
            if 1 <= step <= len(pieces):
                project(pieces[step - 1])
            if step >= 2:
                rectify_on_scalar(pieces[step - 2])

        for half in range(HALVES):
            columns = mean[:, half * BANK : (half + 1) * BANK]
            nc.vector.scalar_tensor_tensor(columns, columns, bias_owed[:], partial[half][:], ADD, ADD)
        for piece in pieces:
            anchor, start, width = piece
            if anchor > SUMMED_BY_TENSOR:
                columns = mean[:, start : start + width]
                nc.vector.scalar_tensor_tensor(columns, pre[piece][:], minus_bias_8th[:], columns, MAX, ADD)
        for half in range(HALVES):
            nc.sync.dma_start(out[:, half * BANK : (half + 1) * BANK], mean[:, half * BANK : (half + 1) * BANK])
